import numpy as np
import ml_dtypes


def mxq(x, axis, fmt="e4m3"):
    dtype, down = {"e4m3": (ml_dtypes.float8_e4m3fn, 7), "e5m2": (ml_dtypes.float8_e5m2, 14)}[fmt]
    v = np.moveaxis(np.asarray(x, np.float32).astype(ml_dtypes.bfloat16).astype(np.float64), axis, -1)
    blocks = v.reshape(v.shape[:-1] + (-1, 32))
    amax = np.abs(blocks).max(-1, keepdims=True)
    byte = np.maximum(np.where(amax > 0, np.frexp(amax)[1] - 1 + 127, 0) - down, 1)
    scale = np.exp2(byte - 127.0)
    codes = (blocks / scale).astype(np.float32).astype(dtype).astype(np.float64)
    return np.moveaxis((codes * scale).reshape(v.shape), -1, axis)


WIDE = False


def mx_kscale(k):
    if not WIDE:
        return np.ones(k)
    levels = np.array([10, -10, 5, -5, 0])
    a = np.random.permutation(np.resize(levels, k // 512 * 4)).reshape(k // 512, 4)
    idx = np.arange(k)
    return np.exp2(a[idx // 512, idx % 128 // 32])


BF16 = ml_dtypes.bfloat16


def bf(x):
    return np.asarray(x, np.float32).astype(BF16)


def f64(x):
    return np.asarray(x).astype(np.float64)


B, C, ROWS, COLS, H, W = 16, 16, 64, 64, 32, 32
K = ROWS * COLS
N = H * W
DENSITY = 0.1


def setup_inputs():
    s = mx_kscale(K)
    image = np.random.standard_normal((B, C, K)) * s
    votes = (np.random.random_sample((K, N)) < DENSITY) * (1.0 + 0.25 * np.random.standard_normal((K, N))) / s[:, None]
    return {"image": bf(image.reshape(B, C, ROWS, COLS)), "vote_index": bf(votes.reshape(ROWS, COLS, H, W))}


def reference(image, vote_index):
    rows, cols, h, w = vote_index.shape
    b, c = image.shape[0], image.shape[1]
    V = f64(vote_index).reshape(rows * cols, h * w)
    x = np.maximum(f64(image).reshape(b * c, rows * cols), 0.0)
    ht = (mxq(x, 1, "e4m3") @ mxq(V, 0, "e4m3")) / cols
    return ht.reshape(b, c, h, w)

@@ -1,0 +1,130 @@
+import concourse.mybir as mybir
+from concourse.masks import make_identity
+
+BF16 = mybir.dt.bfloat16
+F32 = mybir.dt.float32
+U32 = mybir.dt.uint32
+U8 = mybir.dt.uint8
+FP8X4 = mybir.dt.float8_e4m3fn_x4
+
+P = 128
+M = 256
+K = 4096
+N = 1024
+K_PASS = 512
+PASSES = K // K_PASS
+M_TILES = M // P
+HALF = 512
+X_PIECE_K = 2048
+PIECE_PASSES = X_PIECE_K // K_PASS
+
+FLOPS = 2 * M * K * N
+
+
+def tile_ht_kernel(tc, image, vote_index, out):
+    nc = tc.nc
+    x = image.rearrange("b c r q -> (b c) (r q)")
+    votes = vote_index.rearrange("r q h w -> (r q) (h w)")
+    res = out.rearrange("b c h w -> (b c) (h w)")
+
+    with tc.tile_pool(name="keep", bufs=1) as keep, tc.tile_pool(name="stage", bufs=3) as stage, tc.psum_pool(
+        name="accp", bufs=1
+    ) as accp, tc.psum_pool(name="xtp", bufs=4) as xtp, tc.manual_schedule():
+        ident = keep.tile([P, P], F32, name="ident")
+        make_identity(nc, ident[:])
+
+        pieces = [(kh, mt) for kh in range(2) for mt in range(M_TILES)]
+        x_raw = []
+        for i, (kh, mt) in enumerate(pieces):
+            t = keep.tile([P, X_PIECE_K], BF16, name="x_raw%d" % i)
+            nc.sync.dma_start(out=t[:], in_=x[mt * P : (mt + 1) * P, kh * X_PIECE_K : (kh + 1) * X_PIECE_K])
+            x_raw.append(t)
+        v_raw = []
+        for g in range(PASSES):
+            t = keep.tile([P, 4, N], BF16, name="v_raw%d" % g)
+            nc.sync.dma_start(
+                out=t[:].rearrange("p (u e) n -> p u (e n)", u=2),
+                in_=votes[g * K_PASS : (g + 1) * K_PASS, :].rearrange("(u p e) n -> p u (e n)", u=2, e=2),
+            )
+            v_raw.append(t)
+
+        x_codes = keep.tile([P, 4, PIECE_PASSES * P], U32, name="x_codes", align_bytes=64)
+        x_scales = keep.tile([P, 4, PIECE_PASSES * P], U8, name="x_scales", align_bytes=64)
+        v_codes = keep.tile([P, PASSES, N], U32, name="v_codes", align_bytes=64)
+        v_scales = keep.tile([P, PASSES, N], U8, name="v_scales", align_bytes=64)
+        acc = [[accp.tile([P, HALF], F32, name="acc%d%d" % (mt, h)) for h in range(2)] for mt in range(M_TILES)]
+        x_grp = [keep.tile([P, X_PIECE_K], BF16, name="x_grp%d" % i, align_bytes=64) for i in range(4)]
+
+        def x_front(i):
+            pos = keep.tile([P, X_PIECE_K], BF16, name="x_pos%d" % i)
+            nc.vector.tensor_scalar_max(out=pos[:], in0=x_raw[i][:], scalar1=0.0)
+            words = pos[:].bitcast(F32)
+            dst = x_grp[i][:].bitcast(F32).rearrange("p (g m u) -> p g m u", g=PIECE_PASSES, u=2)
+            for b in range(2):
+                xt = xtp.tile([P, 2, 2, P], F32, name="xt", tag="xt")
+                for g2 in range(2):
+                    for u in range(2):
+                        w0 = 256 * (2 * b + g2) + P * u
+                        nc.tensor.transpose(xt[:, g2, u, :], words[:, w0 : w0 + P], ident[:])
+                nc.scalar.copy(out=dst[:, 2 * b : 2 * b + 2, :, :], in_=xt[:].rearrange("p g u m -> p g m u"))
+
+        def x_quant(i):
+            nc.vector.quantize_mx(out=x_codes[:, i, :].bitcast(FP8X4), scales=x_scales[:, i, :], in_=x_grp[i][:])
+
+        grp = {}
+
+        def regroup(g):
+            for h, copy in ((0, nc.vector.tensor_copy), (1, nc.scalar.copy)):
+                t = stage.tile([P, HALF, 4], BF16, name="grp%d" % h, tag="grp%d" % h, align_bytes=64)
+                copy(
+                    out=t[:].rearrange("p (c i) t -> p c t i", i=4),
+                    in_=v_raw[g][:, :, h * HALF : (h + 1) * HALF].rearrange("p t (c i) -> p c t i", i=4),
+                )
+                grp[(g, h)] = t
+
+        def quant_mult(g, h):
+            cols = slice(h * HALF, (h + 1) * HALF)
+            nc.vector.quantize_mx(
+                out=v_codes[:, g, cols].bitcast(FP8X4),
+                scales=v_scales[:, g, cols],
+                in_=grp[(g, h)][:].rearrange("p c t -> p (c t)"),
+            )
+            for mt in range(M_TILES):
+                i = 2 * (g // PIECE_PASSES) + mt
+                rows = slice((g % PIECE_PASSES) * P, (g % PIECE_PASSES + 1) * P)
+                nc.tensor.matmul_mx(
+                    out=acc[mt][h][:],
+                    lhsT=x_codes[:, i, rows].bitcast(FP8X4),
+                    lhsT_scale=x_scales[:, i, rows],
+                    rhs=v_codes[:, g, cols].bitcast(FP8X4),
+                    rhs_scale=v_scales[:, g, cols],
+                    start=(g == 0),
+                    stop=(g == PASSES - 1),
+                )
+
+        x_front(0)
+        x_front(1)
+        x_front(2)
+        x_quant(0)
+        x_front(3)
+        x_quant(1)
+        x_quant(2)
+        regroup(0)
+        x_quant(3)
+        quant_mult(0, 0)
+        for g in range(1, PASSES):
+            regroup(g)
+            quant_mult(g - 1, 1)
+            quant_mult(g, 0)
+        quant_mult(PASSES - 1, 1)
+
+        for h in range(2):
+            for mt in range(M_TILES):
+                o = keep.tile([P, HALF], F32, name="o%d%d" % (mt, h))
+                if mt == 0:
+                    nc.scalar.activation(
+                        out=o[:], in_=acc[mt][h][:], func=mybir.ActivationFunctionType.Copy, scale=1.0 / 64.0
+                    )
+                else:
+                    nc.vector.tensor_scalar_mul(out=o[:], in0=acc[mt][h][:], scalar1=1.0 / 64.0)
+                nc.sync.dma_start(out=res[mt * P : (mt + 1) * P, h * HALF : (h + 1) * HALF], in_=o[:])

@@ -77,8 +77,8 @@ def tile_ht_kernel(tc, image, vote_index, out):
             for h, copy in ((0, nc.vector.tensor_copy), (1, nc.scalar.copy)):
                 t = stage.tile([P, HALF, 4], BF16, name="grp%d" % h, tag="grp%d" % h, align_bytes=64)
                 copy(
-                    out=t[:].rearrange("p (c i) t -> p c t i", i=4),
-                    in_=v_raw[g][:, :, h * HALF : (h + 1) * HALF].rearrange("p t (c i) -> p c t i", i=4),
+                    out=t[:].rearrange("p (c i) t -> p c t i", i=8),
+                    in_=v_raw[g][:, :, h * HALF : (h + 1) * HALF].rearrange("p t (c i) -> p c t i", i=8),
                 )
                 grp[(g, h)] = t
 

import concourse.mybir as mybir
from concourse.masks import make_identity

BF16 = mybir.dt.bfloat16
F32 = mybir.dt.float32
U32 = mybir.dt.uint32
U8 = mybir.dt.uint8
FP8X4 = mybir.dt.float8_e4m3fn_x4

P = 128
M = 256
K = 4096
N = 1024
K_PASS = 512
PASSES = K // K_PASS
M_TILES = M // P
HALF = 512
X_PIECE_K = 2048
PIECE_PASSES = X_PIECE_K // K_PASS

FLOPS = 2 * M * K * N


def tile_ht_kernel(tc, image, vote_index, out):
    nc = tc.nc
    x = image.rearrange("b c r q -> (b c) (r q)")
    votes = vote_index.rearrange("r q h w -> (r q) (h w)")
    res = out.rearrange("b c h w -> (b c) (h w)")

    with tc.tile_pool(name="keep", bufs=1) as keep, tc.tile_pool(name="stage", bufs=3) as stage, tc.psum_pool(
        name="accp", bufs=1
    ) as accp, tc.psum_pool(name="xtp", bufs=4) as xtp, tc.manual_schedule():
        ident = keep.tile([P, P], F32, name="ident")
        make_identity(nc, ident[:])

        pieces = [(kh, mt) for kh in range(2) for mt in range(M_TILES)]
        x_raw = []
        for i, (kh, mt) in enumerate(pieces):
            t = keep.tile([P, X_PIECE_K], BF16, name="x_raw%d" % i)
            nc.sync.dma_start(out=t[:], in_=x[mt * P : (mt + 1) * P, kh * X_PIECE_K : (kh + 1) * X_PIECE_K])
            x_raw.append(t)
        v_raw = []
        for g in range(PASSES):
            t = keep.tile([P, 4, N], BF16, name="v_raw%d" % g)
            nc.sync.dma_start(
                out=t[:].rearrange("p (u e) n -> p u (e n)", u=2),
                in_=votes[g * K_PASS : (g + 1) * K_PASS, :].rearrange("(u p e) n -> p u (e n)", u=2, e=2),
            )
            v_raw.append(t)

        x_codes = keep.tile([P, 4, PIECE_PASSES * P], U32, name="x_codes", align_bytes=64)
        x_scales = keep.tile([P, 4, PIECE_PASSES * P], U8, name="x_scales", align_bytes=64)
        v_codes = keep.tile([P, PASSES, N], U32, name="v_codes", align_bytes=64)
        v_scales = keep.tile([P, PASSES, N], U8, name="v_scales", align_bytes=64)
        acc = [[accp.tile([P, HALF], F32, name="acc%d%d" % (mt, h)) for h in range(2)] for mt in range(M_TILES)]
        x_grp = [keep.tile([P, X_PIECE_K], BF16, name="x_grp%d" % i, align_bytes=64) for i in range(4)]

        def x_front(i):
            pos = keep.tile([P, X_PIECE_K], BF16, name="x_pos%d" % i)
            nc.vector.tensor_scalar_max(out=pos[:], in0=x_raw[i][:], scalar1=0.0)
            words = pos[:].bitcast(F32)
            dst = x_grp[i][:].bitcast(F32).rearrange("p (g m u) -> p g m u", g=PIECE_PASSES, u=2)
            for b in range(2):
                xt = xtp.tile([P, 2, 2, P], F32, name="xt", tag="xt")
                for g2 in range(2):
                    for u in range(2):
                        w0 = 256 * (2 * b + g2) + P * u
                        nc.tensor.transpose(xt[:, g2, u, :], words[:, w0 : w0 + P], ident[:])
                nc.scalar.copy(out=dst[:, 2 * b : 2 * b + 2, :, :], in_=xt[:].rearrange("p g u m -> p g m u"))

        def x_quant(i):
            nc.vector.quantize_mx(out=x_codes[:, i, :].bitcast(FP8X4), scales=x_scales[:, i, :], in_=x_grp[i][:])

        grp = {}

        def regroup(g):
            for h, copy in ((0, nc.vector.tensor_copy), (1, nc.scalar.copy)):
                t = stage.tile([P, HALF, 4], BF16, name="grp%d" % h, tag="grp%d" % h, align_bytes=64)
                copy(
                    out=t[:].rearrange("p (c i) t -> p c t i", i=8),
                    in_=v_raw[g][:, :, h * HALF : (h + 1) * HALF].rearrange("p t (c i) -> p c t i", i=8),
                )
                grp[(g, h)] = t

        def quant_mult(g, h):
            cols = slice(h * HALF, (h + 1) * HALF)
            nc.vector.quantize_mx(
                out=v_codes[:, g, cols].bitcast(FP8X4),
                scales=v_scales[:, g, cols],
                in_=grp[(g, h)][:].rearrange("p c t -> p (c t)"),
            )
            for mt in range(M_TILES):
                i = 2 * (g // PIECE_PASSES) + mt
                rows = slice((g % PIECE_PASSES) * P, (g % PIECE_PASSES + 1) * P)
                nc.tensor.matmul_mx(
                    out=acc[mt][h][:],
                    lhsT=x_codes[:, i, rows].bitcast(FP8X4),
                    lhsT_scale=x_scales[:, i, rows],
                    rhs=v_codes[:, g, cols].bitcast(FP8X4),
                    rhs_scale=v_scales[:, g, cols],
                    start=(g == 0),
                    stop=(g == PASSES - 1),
                )

        x_front(0)
        x_front(1)
        x_front(2)
        x_quant(0)
        x_front(3)
        x_quant(1)
        x_quant(2)
        regroup(0)
        x_quant(3)
        quant_mult(0, 0)
        for g in range(1, PASSES):
            regroup(g)
            quant_mult(g - 1, 1)
            quant_mult(g, 0)
        quant_mult(PASSES - 1, 1)

        for h in range(2):
            for mt in range(M_TILES):
                o = keep.tile([P, HALF], F32, name="o%d%d" % (mt, h))
                if mt == 0:
                    nc.scalar.activation(
                        out=o[:], in_=acc[mt][h][:], func=mybir.ActivationFunctionType.Copy, scale=1.0 / 64.0
                    )
                else:
                    nc.vector.tensor_scalar_mul(out=o[:], in0=acc[mt][h][:], scalar1=1.0 / 64.0)
                nc.sync.dma_start(out=res[mt * P : (mt + 1) * P, h * HALF : (h + 1) * HALF], in_=o[:])
